import numpy as np
import ml_dtypes


def mxq(x, axis, fmt="e4m3"):
    dtype, down = {"e4m3": (ml_dtypes.float8_e4m3fn, 7), "e5m2": (ml_dtypes.float8_e5m2, 14)}[fmt]
    v = np.moveaxis(np.asarray(x, np.float32).astype(ml_dtypes.bfloat16).astype(np.float64), axis, -1)
    blocks = v.reshape(v.shape[:-1] + (-1, 32))
    amax = np.abs(blocks).max(-1, keepdims=True)
    byte = np.maximum(np.where(amax > 0, np.frexp(amax)[1] - 1 + 127, 0) - down, 1)
    scale = np.exp2(byte - 127.0)
    codes = (blocks / scale).astype(np.float32).astype(dtype).astype(np.float64)
    return np.moveaxis((codes * scale).reshape(v.shape), -1, axis)


WIDE = False


def mx_kscale(k):
    if not WIDE:
        return np.ones(k)
    levels = np.array([10, -10, 5, -5, 0])
    if k % 512:
        return np.exp2(np.random.permutation(np.resize(levels, k // 32))).repeat(32)
    a = np.empty((k // 512, 16))
    for p in range(k // 512):
        a[p, :8] = np.random.permutation(np.resize(levels, 8))
        for g in range(8):
            far = levels[np.abs(levels - a[p, g]) >= 10]
            a[p, g + 8] = far[np.random.randint(len(far))]
    return np.exp2(a.ravel()).repeat(32)


BF16 = ml_dtypes.bfloat16


def bf(x):
    return np.asarray(x, np.float32).astype(BF16)


def f64(x):
    return np.asarray(x).astype(np.float64)


B, N, L, H, S, R, C = 4, 1024, 4, 64, 2, 2, 512
M = R * S * H
BN_EPS = 1e-5


def draw0():
    s = mx_kscale(L * M).reshape(L, M)
    t = mx_kscale(C)
    return {"hops": bf((1.7 * np.random.standard_normal((B, N, L, M)) + 0.4 * np.random.standard_normal((L, M))) * s),
            "weight": bf(np.random.standard_normal((L, M, C)) * 0.6 / np.sqrt(L * M) / s[:, :, None]),
            "gamma": bf((1.0 + 0.1 * np.random.standard_normal(C)) * t),
            "beta": bf(0.2 * np.random.standard_normal(C) * t),
            "w2": bf(np.random.standard_normal((C, C)) / np.sqrt(C) / t[None, :]),
            "b2": bf(0.2 * np.random.standard_normal(C))}


def core(hops, weight, gamma, beta, w2, b2):
    hf = f64(hops).reshape(B * N, L * M)
    wm = f64(weight).reshape(L * M, C)
    flat = mxq(hf, 1, "e4m3") @ mxq(wm, 0, "e4m3")
    mean = flat.mean(axis=0)
    var = flat.var(axis=0)
    normed = (flat - mean) * (1.0 / np.sqrt(var + BN_EPS)) * f64(gamma) + f64(beta)
    y = np.maximum(normed, 0.0)
    out = (mxq(y, 1, "e4m3") @ mxq(f64(w2), 1, "e4m3").T) + f64(b2)
    return out.reshape(B, N, C)


def e4m3fn_bytes(y):
    return np.clip(np.asarray(y, np.float64), -448.0, 448.0).astype(np.float32).astype(ml_dtypes.float8_e4m3fn).view(np.uint8)


def e4m3fn_values(b):
    return np.asarray(b, np.uint8).view(ml_dtypes.float8_e4m3fn).astype(np.float64)


def setup_inputs():
    d = draw0()
    x0 = np.asarray(d['w2']).astype(np.float64)
    s = (np.max(np.abs(x0), axis=(0,), keepdims=True) / 448.0).astype(np.float32)
    out = {}
    for k, v in d.items():
        if k == 'w2':
            out['w2_bytes'] = e4m3fn_bytes(x0 / s.astype(np.float64))
            out['w2_scale'] = s
        else:
            out[k] = v
    return out


def reference(hops, weight, gamma, beta, w2_bytes, w2_scale, b2):
    return core(hops, weight, gamma, beta, e4m3fn_values(w2_bytes) * w2_scale.astype(np.float64), b2)

@@ -1,0 +1,321 @@
+from contextlib import ExitStack
+
+import concourse.mybir as mybir
+from concourse.masks import make_identity
+
+F32 = mybir.dt.float32
+BF16 = mybir.dt.bfloat16
+U32 = mybir.dt.uint32
+U8 = mybir.dt.uint8
+FP8 = mybir.dt.float8_e4m3fn
+FP8X4 = mybir.dt.float8_e4m3fn_x4
+ACT = mybir.ActivationFunctionType
+ALU = mybir.AluOpType
+
+P = 128
+ROWS = 4096
+K1 = 1024
+C = 512
+TILE = 512
+TILES = ROWS // TILE
+Q = TILE // P
+HALF = TILE // 2
+PASSES = K1 // 512
+BN_EPS = 1e-5
+LAST = TILES - 1
+
+FLOPS = 2 * ROWS * K1 * C + 2 * ROWS * C * C
+
+
+def tile_ginconvfft_pb_t_kernel(tc, hops, weight, gamma, beta, w2_bytes, w2_scale, b2, out):
+    nc = tc.nc
+    hops_v = hops.rearrange("b n l m -> (b n) (l m)").rearrange("(i p q) k -> i p q k", p=P, q=Q)
+    w_v = weight.rearrange("l m c -> (l m) c").rearrange("(g p j) c -> g p j c", p=P, j=4)
+    out_v = out.rearrange("b n c -> (b n) c").rearrange("(i p q) c -> i p q c", p=P, q=Q)
+
+    with ExitStack() as ctx:
+        keep = ctx.enter_context(tc.tile_pool(name="keep", bufs=1))
+        rawp = ctx.enter_context(tc.tile_pool(name="rawp", bufs=8))
+        work = ctx.enter_context(tc.tile_pool(name="work", bufs=2))
+        codep = ctx.enter_context(tc.tile_pool(name="codep", bufs=3))
+        outp = ctx.enter_context(tc.tile_pool(name="outp", bufs=4))
+        psum = ctx.enter_context(tc.psum_pool(name="psum", bufs=1))
+        ctx.enter_context(tc.manual_schedule())
+
+        ident = keep.tile([P, P], F32, name="ident")
+        make_identity(nc, ident[:])
+        one = keep.tile([P, 1], F32, name="one")
+        nc.vector.memset(one[:], 1.0)
+        warm = keep.tile([P, 1], F32, name="warm")
+        nc.scalar.activation(out=warm[:], in_=one[:], func=ACT.Sqrt)
+
+        raw = {}
+
+        def load_hops(i):
+            for h in range(2):
+                r = rawp.tile([P, 2, K1], BF16, name="raw", tag="raw")
+                nc.sync.dma_start(out=r[:], in_=hops_v[i][:, 2 * h : 2 * h + 2, :])
+                raw[i, h] = r
+
+        load_hops(0)
+        w_raw = []
+        for g in range(PASSES):
+            wr = keep.tile([P, 4, C], BF16, name="w_raw%d" % g)
+            nc.sync.dma_start(out=wr[:], in_=w_v[g])
+            w_raw.append(wr)
+        for i in (1, 2, 3):
+            load_hops(i)
+        w2_codes_in = keep.tile([P, 4, C], U8, name="w2_codes_in")
+        nc.sync.dma_start(out=w2_codes_in[:], in_=w2_bytes.rearrange("(b p) c -> p b c", p=P))
+        w2_sc = keep.tile([P, C], F32, name="w2_sc")
+        nc.sync.dma_start(out=w2_sc[:], in_=w2_scale.rearrange("o k -> (o k)").partition_broadcast(P))
+        b2_all = keep.tile([P, C], BF16, name="b2_all")
+        nc.sync.dma_start(out=b2_all[:], in_=b2.partition_broadcast(P))
+        gam = keep.tile([P, 4], BF16, name="gam")
+        nc.sync.dma_start(out=gam[:], in_=gamma.rearrange("(p t) -> p t", t=4))
+        bet = keep.tile([P, 4], BF16, name="bet")
+        nc.sync.dma_start(out=bet[:], in_=beta.rearrange("(p t) -> p t", t=4))
+        for i in range(4, TILES):
+            load_hops(i)
+
+        w_grp = [keep.tile([P, C, 4], BF16, name="w_grp%d" % g, align_bytes=64) for g in range(PASSES)]
+        w_codes = keep.tile([P, PASSES, C], U32, name="w_codes", align_bytes=64)
+        w_scales = keep.tile([P, PASSES, C], U8, name="w_scales", align_bytes=64)
+        w2_wide = keep.tile([P, 4, C], BF16, name="w2_wide", align_bytes=64)
+        w2_grp = keep.tile([P, C, 4], BF16, name="w2_grp", align_bytes=64)
+        w2_codes = keep.tile([P, C], U32, name="w2_codes", align_bytes=64)
+        w2_scales = keep.tile([P, C], U8, name="w2_scales", align_bytes=64)
+
+        def quantize(codes, scales, grouped):
+            nc.vector.quantize_mx(
+                out=codes.bitcast(FP8X4), scales=scales, in_=grouped.rearrange("p n j -> p (n j)")
+            )
+
+        def group_w(g, copy):
+            copy(
+                out=w_grp[g][:].rearrange("p (t m) j -> p t m j", t=4),
+                in_=w_raw[g][:].rearrange("p j (m t) -> p t m j", t=4),
+            )
+
+        grp = {}
+        codes = {}
+
+        def transpose_bank(j, sources, dst, copy):
+            bank = psum.tile([P, 2, HALF], F32, name="x%d" % j, tag="x%d" % j)
+            for n, words in enumerate(sources):
+                for u in range(2):
+                    nc.tensor.transpose(bank[:, u, n * P : (n + 1) * P], words[:, u : 256 : 2], ident[:])
+            copy(out=dst.bitcast(F32), in_=bank[:].rearrange("p u r -> p r u"))
+
+        def turn(i):
+            grouped = work.tile([P, PASSES, TILE, 4], BF16, name="grouped", tag="grouped", align_bytes=64)
+            grp[i] = grouped
+            for j in range(4):
+                h, g = divmod(j, 2)
+                words = raw[i, h][:].bitcast(F32)
+                transpose_bank(
+                    j,
+                    [words[:, n, 256 * g : 256 * (g + 1)] for n in range(2)],
+                    grouped[:, g, h * HALF : (h + 1) * HALF, :],
+                    nc.vector.tensor_copy if j == 3 else nc.scalar.copy,
+                )
+
+        def quantize_hops(i):
+            hc = codep.tile([P, PASSES, TILE], U32, name="hc", tag="hc", align_bytes=64)
+            hs = codep.tile([P, PASSES, TILE], U8, name="hs", tag="hs", align_bytes=64)
+            for g in range(PASSES):
+                quantize(hc[:, g, :], hs[:, g, :], grp[i][:, g, :, :])
+            codes[i] = (hc, hs)
+
+        def multiply(i, t):
+            z = psum.tile([P, TILE], F32, name="z%d" % t, tag="z%d" % t)
+            hc, hs = codes[i]
+            cols = slice(t * P, (t + 1) * P)
+            for g in range(PASSES):
+                nc.tensor.matmul_mx(
+                    out=z[:],
+                    lhsT=w_codes[:, g, cols].bitcast(FP8X4),
+                    lhsT_scale=w_scales[:, g, cols],
+                    rhs=hc[:, g, :].bitcast(FP8X4),
+                    rhs_scale=hs[:, g, :],
+                    start=(g == 0),
+                    stop=(g == PASSES - 1),
+                )
+            return z
+
+        stats = [keep.tile([P, TILES, 6], F32, name="stats%d" % t) for t in range(4)]
+        zk = {}
+
+        def multiply_and_keep(i):
+            kept = keep.tile([P, 4, TILE], F32, name="zk%d" % i)
+            zk[i] = kept
+            for t in range(4):
+                z = multiply(i, t)
+                nc.scalar.copy(out=kept[:, t, :], in_=z[:])
+                nc.vector.bn_stats(out=stats[t][:, i, :], in_=kept[:, t, :])
+
+        turn(0)
+        quantize_hops(0)
+        group_w(0, nc.scalar.copy)
+        group_w(1, nc.vector.tensor_copy)
+        quantize(w_codes[:, 0, :], w_scales[:, 0, :], w_grp[0][:])
+        quantize(w_codes[:, 1, :], w_scales[:, 1, :], w_grp[1][:])
+        for i in range(1, TILES):
+            turn(i)
+            quantize_hops(i)
+            if i in (5, 6):
+                for b in (2 * (i - 5), 2 * (i - 5) + 1):
+                    nc.vector.tensor_tensor(
+                        out=w2_wide[:, b, :], in0=w2_codes_in[:, b, :].bitcast(FP8), in1=w2_sc[:], op=ALU.mult
+                    )
+            multiply_and_keep(i - 1)
+
+        for j in range(2):
+            words = w2_wide[:].bitcast(F32)
+            transpose_bank(
+                j,
+                [words[:, 2 * j + n, :] for n in range(2)],
+                w2_grp[:, j * HALF : (j + 1) * HALF, :],
+                nc.scalar.copy,
+            )
+        z_last = [multiply(LAST, t) for t in range(4)]
+        quantize(w2_codes[:], w2_scales[:], w2_grp[:])
+
+        mv = [keep.tile([P, 2, 2], F32, name="mv%d" % d) for d in range(2)]
+        sd = [keep.tile([P, 2], F32, name="sd%d" % d) for d in range(2)]
+        rs = [keep.tile([P, 2], F32, name="rs%d" % d) for d in range(2)]
+        aa = [keep.tile([P, 2], F32, name="aa%d" % d) for d in range(2)]
+        ma = [keep.tile([P, 2], F32, name="ma%d" % d) for d in range(2)]
+        bb = [keep.tile([P, 2], F32, name="bb%d" % d) for d in range(2)]
+
+        def stat(t):
+            nc.vector.bn_stats(out=stats[t][:, LAST, :], in_=z_last[t][:])
+
+        def aggregate(t):
+            nc.vector.bn_aggr(out=mv[t // 2][:, t % 2, :], in_=stats[t][:].rearrange("p i s -> p (i s)"))
+
+        def root(d):
+            nc.vector.tensor_scalar(out=rs[d][:], in0=mv[d][:, :, 1], scalar1=BN_EPS, scalar2=None, op0=ALU.add)
+            nc.scalar.activation(out=sd[d][:], in_=rs[d][:], func=ACT.Sqrt)
+
+        inv = [keep.tile([P, 2], F32, name="inv%d" % d) for d in range(2)]
+
+        def recip(d):
+            nc.vector.reciprocal(out=inv[d][:], in_=sd[d][:])
+
+        def factor(d):
+            nc.vector.tensor_tensor(out=aa[d][:], in0=inv[d][:], in1=gam[:, 2 * d : 2 * d + 2], op=ALU.mult)
+
+        def shift1(d):
+            nc.vector.tensor_tensor(out=ma[d][:], in0=mv[d][:, :, 0], in1=aa[d][:], op=ALU.mult)
+
+        def shift2(d):
+            nc.vector.tensor_tensor(out=bb[d][:], in0=bet_f[:, 2 * d : 2 * d + 2], in1=ma[d][:], op=ALU.subtract)
+
+        bet_f = keep.tile([P, 4], F32, name="bet_f")
+        nc.vector.tensor_copy(out=bet_f[:], in_=bet[:])
+
+        def scale_of(t):
+            return aa[t // 2][:, t % 2 : t % 2 + 1]
+
+        def bias_of(t):
+            return bb[t // 2][:, t % 2 : t % 2 + 1]
+
+        y0 = work.tile([P, 4, TILE], BF16, name="y", tag="y", align_bytes=64)
+
+        def norm_v(t):
+            nc.vector.tensor_scalar(
+                out=y0[:, t, 0:HALF], in0=z_last[t][:, 0:HALF],
+                scalar1=scale_of(t), scalar2=bias_of(t), op0=ALU.mult, op1=ALU.add,
+            )
+
+        def norm_s(dst, z, t):
+            nc.scalar.activation(out=dst, in_=z, func=ACT.Relu, bias=bias_of(t), scale=scale_of(t))
+
+        stat(0)
+        aggregate(0)
+        stat(1)
+        aggregate(1)
+        stat(2)
+        root(0)
+        aggregate(2)
+        recip(0)
+        stat(3)
+        factor(0)
+        aggregate(3)
+        shift1(0)
+        root(1)
+        shift2(0)
+        norm_v(0)
+        recip(1)
+        norm_v(1)
+        factor(1)
+        shift1(1)
+        shift2(1)
+        for t in range(4):
+            norm_s(y0[:, t, HALF:TILE], z_last[t][:, HALF:TILE], t)
+        norm_v(2)
+        norm_v(3)
+
+        po = {}
+        ot = {}
+        order = [LAST] + list(range(LAST))
+
+        def group_y(y, h):
+            yg = work.tile([P, HALF, 4], BF16, name="yg%d" % h, tag="yg%d" % h, align_bytes=64)
+            src = y[:, :, h * HALF : (h + 1) * HALF].rearrange("p t n -> p n t")
+            if h == 0:
+                nc.vector.tensor_scalar(out=yg[:], in0=src, scalar1=0.0, scalar2=None, op0=ALU.max)
+            else:
+                nc.scalar.copy(out=yg[:], in_=src)
+            return yg
+
+        def project(i, h, yg):
+            yc = work.tile([P, HALF], U32, name="yc%d" % h, tag="yc%d" % h, align_bytes=64)
+            ys = work.tile([P, HALF], U8, name="ys%d" % h, tag="ys%d" % h, align_bytes=64)
+            quantize(yc[:], ys[:], yg[:])
+            for n in range(2):
+                q = 2 * h + n
+                bank = psum.tile([P, C], F32, name="x%d" % q, tag="x%d" % q)
+                nc.tensor.matmul_mx(
+                    out=bank[:],
+                    lhsT=yc[:, n * P : (n + 1) * P].bitcast(FP8X4),
+                    lhsT_scale=ys[:, n * P : (n + 1) * P],
+                    rhs=w2_codes[:].bitcast(FP8X4),
+                    rhs_scale=w2_scales[:],
+                    start=True,
+                    stop=True,
+                )
+                po[i, q] = bank
+
+        def add_bias(i, q):
+            h, n = divmod(q, 2)
+            if n == 0:
+                ot[i, h] = outp.tile([P, 2, C], F32, name="ot", tag="ot")
+            nc.vector.tensor_tensor(out=ot[i, h][:, n, :], in0=po[i, q][:], in1=b2_all[:], op=ALU.add)
+
+        def store(i, h):
+            nc.sync.dma_start(out=out_v[i][:, 2 * h : 2 * h + 2, :], in_=ot[i, h][:])
+
+        for s, i in enumerate(order):
+            if s == 0:
+                y = y0
+            else:
+                y = work.tile([P, 4, TILE], BF16, name="y", tag="y", align_bytes=64)
+                for t in range(4):
+                    norm_s(y[:, t, :], zk[i][:, t, :], t)
+            yg0 = group_y(y, 0)
+            yg1 = group_y(y, 1)
+            if s > 0:
+                add_bias(order[s - 1], 2)
+            project(i, 0, yg0)
+            if s > 0:
+                add_bias(order[s - 1], 3)
+                store(order[s - 1], 1)
+            project(i, 1, yg1)
+            add_bias(i, 0)
+            add_bias(i, 1)
+            store(i, 0)
+        add_bias(order[-1], 2)
+        add_bias(order[-1], 3)
+        store(order[-1], 1)

@@ -23,6 +23,8 @@ HALF = TILE // 2
 PASSES = K1 // 512
 BN_EPS = 1e-5
 LAST = TILES - 1
+EARLY = 5
+SCALAR_TAKES_MORE = {7}
 
 FLOPS = 2 * ROWS * K1 * C + 2 * ROWS * C * C
 
@@ -54,7 +56,9 @@ def tile_ginconvfft_pb_t_kernel(tc, hops, weight, gamma, beta, w2_bytes, w2_scal
         def load_hops(i):
             for h in range(2):
                 r = rawp.tile([P, 2, K1], BF16, name="raw", tag="raw")
-                nc.sync.dma_start(out=r[:], in_=hops_v[i][:, 2 * h : 2 * h + 2, :])
+                step = 1 if i == 0 else 2
+                for n in range(0, 2, step):
+                    nc.sync.dma_start(out=r[:, n : n + step, :], in_=hops_v[i][:, 2 * h + n : 2 * h + n + step, :])
                 raw[i, h] = r
 
         load_hops(0)
@@ -63,25 +67,27 @@ def tile_ginconvfft_pb_t_kernel(tc, hops, weight, gamma, beta, w2_bytes, w2_scal
             wr = keep.tile([P, 4, C], BF16, name="w_raw%d" % g)
             nc.sync.dma_start(out=wr[:], in_=w_v[g])
             w_raw.append(wr)
-        for i in (1, 2, 3):
-            load_hops(i)
+        gam = keep.tile([P, 4], BF16, name="gam")
+        nc.scalar.dma_start(out=gam[:], in_=gamma.rearrange("(p t) -> p t", t=4))
+        bet = keep.tile([P, 4], BF16, name="bet")
+        nc.scalar.dma_start(out=bet[:], in_=beta.rearrange("(p t) -> p t", t=4))
+        w2_sc = keep.tile([P, 4], F32, name="w2_sc")
+        nc.scalar.dma_start(out=w2_sc[:], in_=w2_scale.rearrange("o (p t) -> p (o t)", t=4))
+        load_hops(1)
         w2_codes_in = keep.tile([P, 4, C], U8, name="w2_codes_in")
         nc.sync.dma_start(out=w2_codes_in[:], in_=w2_bytes.rearrange("(b p) c -> p b c", p=P))
-        w2_sc = keep.tile([P, C], F32, name="w2_sc")
-        nc.sync.dma_start(out=w2_sc[:], in_=w2_scale.rearrange("o k -> (o k)").partition_broadcast(P))
+        for i in range(2, TILES):
+            load_hops(i)
         b2_all = keep.tile([P, C], BF16, name="b2_all")
         nc.sync.dma_start(out=b2_all[:], in_=b2.partition_broadcast(P))
-        gam = keep.tile([P, 4], BF16, name="gam")
-        nc.sync.dma_start(out=gam[:], in_=gamma.rearrange("(p t) -> p t", t=4))
-        bet = keep.tile([P, 4], BF16, name="bet")
-        nc.sync.dma_start(out=bet[:], in_=beta.rearrange("(p t) -> p t", t=4))
-        for i in range(4, TILES):
-            load_hops(i)
+        ngam = keep.tile([P, 4], F32, name="ngam")
+        bet_f = keep.tile([P, 4], F32, name="bet_f")
 
         w_grp = [keep.tile([P, C, 4], BF16, name="w_grp%d" % g, align_bytes=64) for g in range(PASSES)]
         w_codes = keep.tile([P, PASSES, C], U32, name="w_codes", align_bytes=64)
         w_scales = keep.tile([P, PASSES, C], U8, name="w_scales", align_bytes=64)
         w2_wide = keep.tile([P, 4, C], BF16, name="w2_wide", align_bytes=64)
+        w2_turned = keep.tile([P, C, 4], BF16, name="w2_turned", align_bytes=64)
         w2_grp = keep.tile([P, C, 4], BF16, name="w2_grp", align_bytes=64)
         w2_codes = keep.tile([P, C], U32, name="w2_codes", align_bytes=64)
         w2_scales = keep.tile([P, C], U8, name="w2_scales", align_bytes=64)
@@ -117,7 +123,7 @@ def tile_ginconvfft_pb_t_kernel(tc, hops, weight, gamma, beta, w2_bytes, w2_scal
                     j,
                     [words[:, n, 256 * g : 256 * (g + 1)] for n in range(2)],
                     grouped[:, g, h * HALF : (h + 1) * HALF, :],
-                    nc.vector.tensor_copy if j == 3 else nc.scalar.copy,
+                    nc.vector.tensor_copy if j == 3 and i < 5 else nc.scalar.copy,
                 )
 
         def quantize_hops(i):
@@ -143,7 +149,16 @@ def tile_ginconvfft_pb_t_kernel(tc, hops, weight, gamma, beta, w2_bytes, w2_scal
                 )
             return z
 
-        stats = [keep.tile([P, TILES, 6], F32, name="stats%d" % t) for t in range(4)]
+        stats = [keep.tile([P, EARLY, 6], F32, name="stats%d" % t) for t in range(4)]
+        tail_stats = [keep.tile([P, 3 + 6 * (TILES - EARLY)], F32, name="tail_stats%d" % t) for t in range(4)]
+        for t in range(4):
+            nc.vector.memset(tail_stats[t][:, 0:1], float(EARLY * TILE))
+
+        def stats_of(t, i):
+            if i < EARLY:
+                return stats[t][:, i, :]
+            return tail_stats[t][:, 3 + 6 * (i - EARLY) : 9 + 6 * (i - EARLY)]
+
         zk = {}
 
         def multiply_and_keep(i):
@@ -152,7 +167,17 @@ def tile_ginconvfft_pb_t_kernel(tc, hops, weight, gamma, beta, w2_bytes, w2_scal
             for t in range(4):
                 z = multiply(i, t)
                 nc.scalar.copy(out=kept[:, t, :], in_=z[:])
-                nc.vector.bn_stats(out=stats[t][:, i, :], in_=kept[:, t, :])
+                nc.vector.bn_stats(out=stats_of(t, i), in_=kept[:, t, :])
+
+        def widen(b, copy):
+            copy(out=w2_wide[:, b, :], in_=w2_codes_in[:, b, :].bitcast(FP8))
+
+        def scale_w2(b):
+            rows = slice(b * P, (b + 1) * P)
+            nc.vector.tensor_tensor(
+                out=w2_grp[:, rows, :], in0=w2_turned[:, rows, :],
+                in1=w2_sc[:].unsqueeze(1).to_broadcast([P, P, 4]), op=ALU.mult,
+            )
 
         turn(0)
         quantize_hops(0)
@@ -162,58 +187,65 @@ def tile_ginconvfft_pb_t_kernel(tc, hops, weight, gamma, beta, w2_bytes, w2_scal
         quantize(w_codes[:, 1, :], w_scales[:, 1, :], w_grp[1][:])
         for i in range(1, TILES):
             turn(i)
-            quantize_hops(i)
-            if i in (5, 6):
-                for b in (2 * (i - 5), 2 * (i - 5) + 1):
-                    nc.vector.tensor_tensor(
-                        out=w2_wide[:, b, :], in0=w2_codes_in[:, b, :].bitcast(FP8), in1=w2_sc[:], op=ALU.mult
+            if i > EARLY:
+                pair = (0, 1) if i == EARLY + 1 else (2, 3)
+                for t in pair:
+                    nc.vector.bn_aggr(out=tail_stats[t][:, 1:3], in_=stats[t][:].rearrange("p i s -> p (i s)"))
+                for t in pair:
+                    nc.vector.tensor_scalar(
+                        out=tail_stats[t][:, 2:3], in0=tail_stats[t][:, 2:3],
+                        scalar1=float(EARLY * TILE), scalar2=None, op0=ALU.mult,
                     )
+            quantize_hops(i)
+            if i in (1, 2):
+                widen(2 * i - 2, nc.vector.tensor_copy)
+                widen(2 * i - 1, nc.scalar.copy)
+            if i == 3:
+                scale_w2(0)
+                scale_w2(1)
+            if i == 4:
+                scale_w2(2)
+            if i == 5:
+                scale_w2(3)
+            if i == 5:
+                nc.vector.tensor_scalar(out=ngam[:], in0=gam[:], scalar1=-1.0, scalar2=None, op0=ALU.mult)
+                nc.vector.tensor_copy(out=bet_f[:], in_=bet[:])
+            if i == 6:
+                quantize(w2_codes[:], w2_scales[:], w2_grp[:])
             multiply_and_keep(i - 1)
+            if i == 2:
+                for j in range(2):
+                    words = w2_wide[:].bitcast(F32)
+                    transpose_bank(
+                        j + 2,
+                        [words[:, 2 * j + n, :] for n in range(2)],
+                        w2_turned[:, j * HALF : (j + 1) * HALF, :],
+                        nc.scalar.copy,
+                    )
 
-        for j in range(2):
-            words = w2_wide[:].bitcast(F32)
-            transpose_bank(
-                j,
-                [words[:, 2 * j + n, :] for n in range(2)],
-                w2_grp[:, j * HALF : (j + 1) * HALF, :],
-                nc.scalar.copy,
-            )
         z_last = [multiply(LAST, t) for t in range(4)]
-        quantize(w2_codes[:], w2_scales[:], w2_grp[:])
 
         mv = [keep.tile([P, 2, 2], F32, name="mv%d" % d) for d in range(2)]
         sd = [keep.tile([P, 2], F32, name="sd%d" % d) for d in range(2)]
-        rs = [keep.tile([P, 2], F32, name="rs%d" % d) for d in range(2)]
+        inv = [keep.tile([P, 2], F32, name="inv%d" % d) for d in range(2)]
         aa = [keep.tile([P, 2], F32, name="aa%d" % d) for d in range(2)]
-        ma = [keep.tile([P, 2], F32, name="ma%d" % d) for d in range(2)]
+        mg = [keep.tile([P, 2], F32, name="mg%d" % d) for d in range(2)]
         bb = [keep.tile([P, 2], F32, name="bb%d" % d) for d in range(2)]
 
         def stat(t):
-            nc.vector.bn_stats(out=stats[t][:, LAST, :], in_=z_last[t][:])
+            nc.vector.bn_stats(out=stats_of(t, LAST), in_=z_last[t][:])
 
         def aggregate(t):
-            nc.vector.bn_aggr(out=mv[t // 2][:, t % 2, :], in_=stats[t][:].rearrange("p i s -> p (i s)"))
+            nc.vector.bn_aggr(out=mv[t // 2][:, t % 2, :], in_=tail_stats[t][:])
 
         def root(d):
-            nc.vector.tensor_scalar(out=rs[d][:], in0=mv[d][:, :, 1], scalar1=BN_EPS, scalar2=None, op0=ALU.add)
-            nc.scalar.activation(out=sd[d][:], in_=rs[d][:], func=ACT.Sqrt)
+            nc.scalar.activation(out=sd[d][:], in_=mv[d][:, :, 1], func=ACT.Sqrt, bias=BN_EPS)
 
-        inv = [keep.tile([P, 2], F32, name="inv%d" % d) for d in range(2)]
+        def shift(d):
+            nc.vector.tensor_tensor(out=mg[d][:], in0=mv[d][:, :, 0], in1=ngam[:, 2 * d : 2 * d + 2], op=ALU.mult)
 
         def recip(d):
             nc.vector.reciprocal(out=inv[d][:], in_=sd[d][:])
-
-        def factor(d):
-            nc.vector.tensor_tensor(out=aa[d][:], in0=inv[d][:], in1=gam[:, 2 * d : 2 * d + 2], op=ALU.mult)
-
-        def shift1(d):
-            nc.vector.tensor_tensor(out=ma[d][:], in0=mv[d][:, :, 0], in1=aa[d][:], op=ALU.mult)
-
-        def shift2(d):
-            nc.vector.tensor_tensor(out=bb[d][:], in0=bet_f[:, 2 * d : 2 * d + 2], in1=ma[d][:], op=ALU.subtract)
-
-        bet_f = keep.tile([P, 4], F32, name="bet_f")
-        nc.vector.tensor_copy(out=bet_f[:], in_=bet[:])
 
         def scale_of(t):
             return aa[t // 2][:, t % 2 : t % 2 + 1]
@@ -221,101 +253,151 @@ def tile_ginconvfft_pb_t_kernel(tc, hops, weight, gamma, beta, w2_bytes, w2_scal
         def bias_of(t):
             return bb[t // 2][:, t % 2 : t % 2 + 1]
 
-        y0 = work.tile([P, 4, TILE], BF16, name="y", tag="y", align_bytes=64)
+        def factors(d):
+            nc.vector.tensor_tensor(out=aa[d][:], in0=inv[d][:], in1=gam[:, 2 * d : 2 * d + 2], op=ALU.mult)
+            for n in range(2):
+                nc.vector.scalar_tensor_tensor(
+                    out=bb[d][:, n : n + 1], in0=mg[d][:, n : n + 1], scalar=inv[d][:, n : n + 1],
+                    in1=bet_f[:, 2 * d + n : 2 * d + n + 1], op0=ALU.mult, op1=ALU.add,
+                )
 
-        def norm_v(t):
+        def norm_v(dst, z, t):
             nc.vector.tensor_scalar(
-                out=y0[:, t, 0:HALF], in0=z_last[t][:, 0:HALF],
-                scalar1=scale_of(t), scalar2=bias_of(t), op0=ALU.mult, op1=ALU.add,
+                out=dst, in0=z, scalar1=scale_of(t), scalar2=bias_of(t), op0=ALU.mult, op1=ALU.add
             )
 
         def norm_s(dst, z, t):
             nc.scalar.activation(out=dst, in_=z, func=ACT.Relu, bias=bias_of(t), scale=scale_of(t))
 
-        stat(0)
-        aggregate(0)
-        stat(1)
-        aggregate(1)
-        stat(2)
-        root(0)
-        aggregate(2)
-        recip(0)
-        stat(3)
-        factor(0)
-        aggregate(3)
-        shift1(0)
-        root(1)
-        shift2(0)
-        norm_v(0)
-        recip(1)
-        norm_v(1)
-        factor(1)
-        shift1(1)
-        shift2(1)
-        for t in range(4):
-            norm_s(y0[:, t, HALF:TILE], z_last[t][:, HALF:TILE], t)
-        norm_v(2)
-        norm_v(3)
-
+        order = [LAST] + list(range(LAST))
+        y_tiles = {}
+        yg = {}
+        yq = {}
         po = {}
         ot = {}
-        order = [LAST] + list(range(LAST))
+        halves = [slice(0, HALF), slice(HALF, TILE)]
 
-        def group_y(y, h):
-            yg = work.tile([P, HALF, 4], BF16, name="yg%d" % h, tag="yg%d" % h, align_bytes=64)
-            src = y[:, :, h * HALF : (h + 1) * HALF].rearrange("p t n -> p n t")
-            if h == 0:
-                nc.vector.tensor_scalar(out=yg[:], in0=src, scalar1=0.0, scalar2=None, op0=ALU.max)
-            else:
-                nc.scalar.copy(out=yg[:], in_=src)
-            return yg
+        def new_y(s):
+            y = work.tile([P, 4, TILE], BF16, name="y", tag="y", align_bytes=64)
+            y_tiles[s] = y
 
-        def project(i, h, yg):
+        def norm(s, t, on, cols=slice(0, TILE)):
+            if s < TILES:
+                z = z_last[t] if s == 0 else zk[order[s]][:, t, :]
+                on(y_tiles[s][:, t, cols], z[:, cols], t)
+
+        def group_y(s, h):
+            if (s, h) not in yg:
+                g = work.tile([P, HALF, 4], BF16, name="yg%d" % h, tag="yg%d" % h, align_bytes=64)
+                yg[s, h] = g
+            return yg[s, h]
+
+        def group_on_vector(s, lo, hi):
+            src = y_tiles[s][:, :, lo:hi].rearrange("p t (c i) -> p c t i", i=4)
+            dst = group_y(s, 0)[:, lo:hi, :].rearrange("p (c i) t -> p c t i", i=4)
+            nc.vector.tensor_scalar(out=dst, in0=src, scalar1=0.0, scalar2=None, op0=ALU.max)
+
+        def group_on_scalar(s, lo, hi):
+            src = y_tiles[s][:, :, lo:hi].rearrange("p t (c i) -> p c t i", i=4)
+            h = lo // HALF
+            dst = group_y(s, h)[:, lo - h * HALF : hi - h * HALF, :].rearrange("p (c i) t -> p c t i", i=4)
+            nc.scalar.copy(out=dst, in_=src)
+
+        def quantize_y(s, h):
             yc = work.tile([P, HALF], U32, name="yc%d" % h, tag="yc%d" % h, align_bytes=64)
             ys = work.tile([P, HALF], U8, name="ys%d" % h, tag="ys%d" % h, align_bytes=64)
-            quantize(yc[:], ys[:], yg[:])
-            for n in range(2):
-                q = 2 * h + n
-                bank = psum.tile([P, C], F32, name="x%d" % q, tag="x%d" % q)
-                nc.tensor.matmul_mx(
-                    out=bank[:],
-                    lhsT=yc[:, n * P : (n + 1) * P].bitcast(FP8X4),
-                    lhsT_scale=ys[:, n * P : (n + 1) * P],
-                    rhs=w2_codes[:].bitcast(FP8X4),
-                    rhs_scale=w2_scales[:],
-                    start=True,
-                    stop=True,
-                )
-                po[i, q] = bank
+            quantize(yc[:], ys[:], yg[s, h][:])
+            yq[s, h] = (yc, ys)
 
-        def add_bias(i, q):
+        def project(s, q):
+            h, n = divmod(q, 2)
+            yc, ys = yq[s, h]
+            bank = psum.tile([P, C], F32, name="x%d" % q, tag="x%d" % q)
+            nc.tensor.matmul_mx(
+                out=bank[:],
+                lhsT=yc[:, n * P : (n + 1) * P].bitcast(FP8X4),
+                lhsT_scale=ys[:, n * P : (n + 1) * P],
+                rhs=w2_codes[:].bitcast(FP8X4),
+                rhs_scale=w2_scales[:],
+                start=True,
+                stop=True,
+            )
+            po[s, q] = bank
+
+        def add_bias(s, q):
             h, n = divmod(q, 2)
             if n == 0:
-                ot[i, h] = outp.tile([P, 2, C], F32, name="ot", tag="ot")
-            nc.vector.tensor_tensor(out=ot[i, h][:, n, :], in0=po[i, q][:], in1=b2_all[:], op=ALU.add)
+                o = outp.tile([P, 2, C], F32, name="ot", tag="ot")
+                ot[s, h] = o
+            nc.vector.tensor_tensor(out=ot[s, h][:, n, :], in0=po[s, q][:], in1=b2_all[:], op=ALU.add)
+            if s == TILES - 1:
+                nc.sync.dma_start(out=out_v[order[s]][:, q : q + 1, :], in_=ot[s, h][:, n : n + 1, :])
+            elif n == 1:
+                nc.sync.dma_start(out=out_v[order[s]][:, 2 * h : 2 * h + 2, :], in_=ot[s, h][:])
 
-        def store(i, h):
-            nc.sync.dma_start(out=out_v[i][:, 2 * h : 2 * h + 2, :], in_=ot[i, h][:])
+        stat(0)
+        stat(1)
+        aggregate(0)
+        aggregate(1)
+        root(0)
+        stat(2)
+        shift(0)
+        recip(0)
+        stat(3)
+        factors(0)
+        aggregate(2)
+        aggregate(3)
+        root(1)
+        new_y(0)
+        new_y(1)
+        norm(0, 0, norm_s)
+        norm(0, 1, norm_s)
+        norm(1, 0, norm_v, halves[0])
+        shift(1)
+        recip(1)
+        norm(1, 1, norm_v, halves[0])
+        factors(1)
+        for t in (2, 3):
+            norm(0, t, norm_v, halves[0])
+            norm(0, t, norm_s, halves[1])
 
-        for s, i in enumerate(order):
-            if s == 0:
-                y = y0
-            else:
-                y = work.tile([P, 4, TILE], BF16, name="y", tag="y", align_bytes=64)
-                for t in range(4):
-                    norm_s(y[:, t, :], zk[i][:, t, :], t)
-            yg0 = group_y(y, 0)
-            yg1 = group_y(y, 1)
-            if s > 0:
-                add_bias(order[s - 1], 2)
-            project(i, 0, yg0)
-            if s > 0:
-                add_bias(order[s - 1], 3)
-                store(order[s - 1], 1)
-            project(i, 1, yg1)
-            add_bias(i, 0)
-            add_bias(i, 1)
-            store(i, 0)
-        add_bias(order[-1], 2)
-        add_bias(order[-1], 3)
-        store(order[-1], 1)
+        group_on_scalar(0, HALF, TILE)
+        norm(1, 2, norm_v, halves[0])
+        group_on_vector(0, 0, HALF)
+        norm(1, 3, norm_v, halves[0])
+        for t in range(4):
+            norm(1, t, norm_s, halves[1])
+        quantize_y(0, 0)
+        project(0, 0)
+        project(0, 1)
+        group_on_vector(1, 0, HALF)
+        quantize_y(0, 1)
+        project(0, 2)
+        project(0, 3)
+        add_bias(0, 0)
+        add_bias(0, 1)
+
+        for s in range(1, TILES):
+            if s + 1 < TILES:
+                new_y(s + 1)
+            if s in SCALAR_TAKES_MORE:
+                group_on_scalar(s, P, HALF)
+            norm(s + 1, 0, norm_s)
+            norm(s + 1, 1, norm_s)
+            group_on_scalar(s, HALF, TILE)
+            norm(s + 1, 2, norm_s)
+            norm(s + 1, 3, norm_s)
+            if s > 1:
+                group_on_vector(s, 0, P if s in SCALAR_TAKES_MORE else HALF)
+            add_bias(s - 1, 2)
+            quantize_y(s, 0)
+            project(s, 0)
+            project(s, 1)
+            add_bias(s - 1, 3)
+            add_bias(s, 0)
+            quantize_y(s, 1)
+            project(s, 2)
+            project(s, 3)
+            add_bias(s, 1)
+        add_bias(TILES - 1, 2)
+        add_bias(TILES - 1, 3)

@@ -24,7 +24,7 @@ PASSES = K1 // 512
 BN_EPS = 1e-5
 LAST = TILES - 1
 EARLY = 5
-SCALAR_TAKES_MORE = {7}
+SCALAR_TAKES_MORE = {99}
 
 FLOPS = 2 * ROWS * K1 * C + 2 * ROWS * C * C
 
@@ -380,24 +380,21 @@ def tile_ginconvfft_pb_t_kernel(tc, hops, weight, gamma, beta, w2_bytes, w2_scal
         for s in range(1, TILES):
             if s + 1 < TILES:
                 new_y(s + 1)
-            if s in SCALAR_TAKES_MORE:
-                group_on_scalar(s, P, HALF)
             norm(s + 1, 0, norm_s)
-            norm(s + 1, 1, norm_s)
             group_on_scalar(s, HALF, TILE)
-            norm(s + 1, 2, norm_s)
-            norm(s + 1, 3, norm_s)
+            for t in range(1, 4):
+                norm(s + 1, t, norm_s)
             if s > 1:
-                group_on_vector(s, 0, P if s in SCALAR_TAKES_MORE else HALF)
+                group_on_vector(s, 0, HALF)
             add_bias(s - 1, 2)
             quantize_y(s, 0)
             project(s, 0)
             project(s, 1)
             add_bias(s - 1, 3)
-            add_bias(s, 0)
             quantize_y(s, 1)
             project(s, 2)
             project(s, 3)
+            add_bias(s, 0)
             add_bias(s, 1)
         add_bias(TILES - 1, 2)
         add_bias(TILES - 1, 3)

from contextlib import ExitStack

import concourse.mybir as mybir
from concourse.masks import make_identity

F32 = mybir.dt.float32
BF16 = mybir.dt.bfloat16
U32 = mybir.dt.uint32
U8 = mybir.dt.uint8
FP8 = mybir.dt.float8_e4m3fn
FP8X4 = mybir.dt.float8_e4m3fn_x4
ACT = mybir.ActivationFunctionType
ALU = mybir.AluOpType

P = 128
ROWS = 4096
K1 = 1024
C = 512
TILE = 512
TILES = ROWS // TILE
Q = TILE // P
HALF = TILE // 2
PASSES = K1 // 512
BN_EPS = 1e-5
LAST = TILES - 1
EARLY = 5
SCALAR_TAKES_MORE = {99}

FLOPS = 2 * ROWS * K1 * C + 2 * ROWS * C * C


def tile_ginconvfft_pb_t_kernel(tc, hops, weight, gamma, beta, w2_bytes, w2_scale, b2, out):
    nc = tc.nc
    hops_v = hops.rearrange("b n l m -> (b n) (l m)").rearrange("(i p q) k -> i p q k", p=P, q=Q)
    w_v = weight.rearrange("l m c -> (l m) c").rearrange("(g p j) c -> g p j c", p=P, j=4)
    out_v = out.rearrange("b n c -> (b n) c").rearrange("(i p q) c -> i p q c", p=P, q=Q)

    with ExitStack() as ctx:
        keep = ctx.enter_context(tc.tile_pool(name="keep", bufs=1))
        rawp = ctx.enter_context(tc.tile_pool(name="rawp", bufs=8))
        work = ctx.enter_context(tc.tile_pool(name="work", bufs=2))
        codep = ctx.enter_context(tc.tile_pool(name="codep", bufs=3))
        outp = ctx.enter_context(tc.tile_pool(name="outp", bufs=4))
        psum = ctx.enter_context(tc.psum_pool(name="psum", bufs=1))
        ctx.enter_context(tc.manual_schedule())

        ident = keep.tile([P, P], F32, name="ident")
        make_identity(nc, ident[:])
        one = keep.tile([P, 1], F32, name="one")
        nc.vector.memset(one[:], 1.0)
        warm = keep.tile([P, 1], F32, name="warm")
        nc.scalar.activation(out=warm[:], in_=one[:], func=ACT.Sqrt)

        raw = {}

        def load_hops(i):
            for h in range(2):
                r = rawp.tile([P, 2, K1], BF16, name="raw", tag="raw")
                step = 1 if i == 0 else 2
                for n in range(0, 2, step):
                    nc.sync.dma_start(out=r[:, n : n + step, :], in_=hops_v[i][:, 2 * h + n : 2 * h + n + step, :])
                raw[i, h] = r

        load_hops(0)
        w_raw = []
        for g in range(PASSES):
            wr = keep.tile([P, 4, C], BF16, name="w_raw%d" % g)
            nc.sync.dma_start(out=wr[:], in_=w_v[g])
            w_raw.append(wr)
        gam = keep.tile([P, 4], BF16, name="gam")
        nc.scalar.dma_start(out=gam[:], in_=gamma.rearrange("(p t) -> p t", t=4))
        bet = keep.tile([P, 4], BF16, name="bet")
        nc.scalar.dma_start(out=bet[:], in_=beta.rearrange("(p t) -> p t", t=4))
        w2_sc = keep.tile([P, 4], F32, name="w2_sc")
        nc.scalar.dma_start(out=w2_sc[:], in_=w2_scale.rearrange("o (p t) -> p (o t)", t=4))
        load_hops(1)
        w2_codes_in = keep.tile([P, 4, C], U8, name="w2_codes_in")
        nc.sync.dma_start(out=w2_codes_in[:], in_=w2_bytes.rearrange("(b p) c -> p b c", p=P))
        for i in range(2, TILES):
            load_hops(i)
        b2_all = keep.tile([P, C], BF16, name="b2_all")
        nc.sync.dma_start(out=b2_all[:], in_=b2.partition_broadcast(P))
        ngam = keep.tile([P, 4], F32, name="ngam")
        bet_f = keep.tile([P, 4], F32, name="bet_f")

        w_grp = [keep.tile([P, C, 4], BF16, name="w_grp%d" % g, align_bytes=64) for g in range(PASSES)]
        w_codes = keep.tile([P, PASSES, C], U32, name="w_codes", align_bytes=64)
        w_scales = keep.tile([P, PASSES, C], U8, name="w_scales", align_bytes=64)
        w2_wide = keep.tile([P, 4, C], BF16, name="w2_wide", align_bytes=64)
        w2_turned = keep.tile([P, C, 4], BF16, name="w2_turned", align_bytes=64)
        w2_grp = keep.tile([P, C, 4], BF16, name="w2_grp", align_bytes=64)
        w2_codes = keep.tile([P, C], U32, name="w2_codes", align_bytes=64)
        w2_scales = keep.tile([P, C], U8, name="w2_scales", align_bytes=64)

        def quantize(codes, scales, grouped):
            nc.vector.quantize_mx(
                out=codes.bitcast(FP8X4), scales=scales, in_=grouped.rearrange("p n j -> p (n j)")
            )

        def group_w(g, copy):
            copy(
                out=w_grp[g][:].rearrange("p (t m) j -> p t m j", t=4),
                in_=w_raw[g][:].rearrange("p j (m t) -> p t m j", t=4),
            )

        grp = {}
        codes = {}

        def transpose_bank(j, sources, dst, copy):
            bank = psum.tile([P, 2, HALF], F32, name="x%d" % j, tag="x%d" % j)
            for n, words in enumerate(sources):
                for u in range(2):
                    nc.tensor.transpose(bank[:, u, n * P : (n + 1) * P], words[:, u : 256 : 2], ident[:])
            copy(out=dst.bitcast(F32), in_=bank[:].rearrange("p u r -> p r u"))

        def turn(i):
            grouped = work.tile([P, PASSES, TILE, 4], BF16, name="grouped", tag="grouped", align_bytes=64)
            grp[i] = grouped
            for j in range(4):
                h, g = divmod(j, 2)
                words = raw[i, h][:].bitcast(F32)
                transpose_bank(
                    j,
                    [words[:, n, 256 * g : 256 * (g + 1)] for n in range(2)],
                    grouped[:, g, h * HALF : (h + 1) * HALF, :],
                    nc.vector.tensor_copy if j == 3 and i < 5 else nc.scalar.copy,
                )

        def quantize_hops(i):
            hc = codep.tile([P, PASSES, TILE], U32, name="hc", tag="hc", align_bytes=64)
            hs = codep.tile([P, PASSES, TILE], U8, name="hs", tag="hs", align_bytes=64)
            for g in range(PASSES):
                quantize(hc[:, g, :], hs[:, g, :], grp[i][:, g, :, :])
            codes[i] = (hc, hs)

        def multiply(i, t):
            z = psum.tile([P, TILE], F32, name="z%d" % t, tag="z%d" % t)
            hc, hs = codes[i]
            cols = slice(t * P, (t + 1) * P)
            for g in range(PASSES):
                nc.tensor.matmul_mx(
                    out=z[:],
                    lhsT=w_codes[:, g, cols].bitcast(FP8X4),
                    lhsT_scale=w_scales[:, g, cols],
                    rhs=hc[:, g, :].bitcast(FP8X4),
                    rhs_scale=hs[:, g, :],
                    start=(g == 0),
                    stop=(g == PASSES - 1),
                )
            return z

        stats = [keep.tile([P, EARLY, 6], F32, name="stats%d" % t) for t in range(4)]
        tail_stats = [keep.tile([P, 3 + 6 * (TILES - EARLY)], F32, name="tail_stats%d" % t) for t in range(4)]
        for t in range(4):
            nc.vector.memset(tail_stats[t][:, 0:1], float(EARLY * TILE))

        def stats_of(t, i):
            if i < EARLY:
                return stats[t][:, i, :]
            return tail_stats[t][:, 3 + 6 * (i - EARLY) : 9 + 6 * (i - EARLY)]

        zk = {}

        def multiply_and_keep(i):
            kept = keep.tile([P, 4, TILE], F32, name="zk%d" % i)
            zk[i] = kept
            for t in range(4):
                z = multiply(i, t)
                nc.scalar.copy(out=kept[:, t, :], in_=z[:])
                nc.vector.bn_stats(out=stats_of(t, i), in_=kept[:, t, :])

        def widen(b, copy):
            copy(out=w2_wide[:, b, :], in_=w2_codes_in[:, b, :].bitcast(FP8))

        def scale_w2(b):
            rows = slice(b * P, (b + 1) * P)
            nc.vector.tensor_tensor(
                out=w2_grp[:, rows, :], in0=w2_turned[:, rows, :],
                in1=w2_sc[:].unsqueeze(1).to_broadcast([P, P, 4]), op=ALU.mult,
            )

        turn(0)
        quantize_hops(0)
        group_w(0, nc.scalar.copy)
        group_w(1, nc.vector.tensor_copy)
        quantize(w_codes[:, 0, :], w_scales[:, 0, :], w_grp[0][:])
        quantize(w_codes[:, 1, :], w_scales[:, 1, :], w_grp[1][:])
        for i in range(1, TILES):
            turn(i)
            if i > EARLY:
                pair = (0, 1) if i == EARLY + 1 else (2, 3)
                for t in pair:
                    nc.vector.bn_aggr(out=tail_stats[t][:, 1:3], in_=stats[t][:].rearrange("p i s -> p (i s)"))
                for t in pair:
                    nc.vector.tensor_scalar(
                        out=tail_stats[t][:, 2:3], in0=tail_stats[t][:, 2:3],
                        scalar1=float(EARLY * TILE), scalar2=None, op0=ALU.mult,
                    )
            quantize_hops(i)
            if i in (1, 2):
                widen(2 * i - 2, nc.vector.tensor_copy)
                widen(2 * i - 1, nc.scalar.copy)
            if i == 3:
                scale_w2(0)
                scale_w2(1)
            if i == 4:
                scale_w2(2)
            if i == 5:
                scale_w2(3)
            if i == 5:
                nc.vector.tensor_scalar(out=ngam[:], in0=gam[:], scalar1=-1.0, scalar2=None, op0=ALU.mult)
                nc.vector.tensor_copy(out=bet_f[:], in_=bet[:])
            if i == 6:
                quantize(w2_codes[:], w2_scales[:], w2_grp[:])
            multiply_and_keep(i - 1)
            if i == 2:
                for j in range(2):
                    words = w2_wide[:].bitcast(F32)
                    transpose_bank(
                        j + 2,
                        [words[:, 2 * j + n, :] for n in range(2)],
                        w2_turned[:, j * HALF : (j + 1) * HALF, :],
                        nc.scalar.copy,
                    )

        z_last = [multiply(LAST, t) for t in range(4)]

        mv = [keep.tile([P, 2, 2], F32, name="mv%d" % d) for d in range(2)]
        sd = [keep.tile([P, 2], F32, name="sd%d" % d) for d in range(2)]
        inv = [keep.tile([P, 2], F32, name="inv%d" % d) for d in range(2)]
        aa = [keep.tile([P, 2], F32, name="aa%d" % d) for d in range(2)]
        mg = [keep.tile([P, 2], F32, name="mg%d" % d) for d in range(2)]
        bb = [keep.tile([P, 2], F32, name="bb%d" % d) for d in range(2)]

        def stat(t):
            nc.vector.bn_stats(out=stats_of(t, LAST), in_=z_last[t][:])

        def aggregate(t):
            nc.vector.bn_aggr(out=mv[t // 2][:, t % 2, :], in_=tail_stats[t][:])

        def root(d):
            nc.scalar.activation(out=sd[d][:], in_=mv[d][:, :, 1], func=ACT.Sqrt, bias=BN_EPS)

        def shift(d):
            nc.vector.tensor_tensor(out=mg[d][:], in0=mv[d][:, :, 0], in1=ngam[:, 2 * d : 2 * d + 2], op=ALU.mult)

        def recip(d):
            nc.vector.reciprocal(out=inv[d][:], in_=sd[d][:])

        def scale_of(t):
            return aa[t // 2][:, t % 2 : t % 2 + 1]

        def bias_of(t):
            return bb[t // 2][:, t % 2 : t % 2 + 1]

        def factors(d):
            nc.vector.tensor_tensor(out=aa[d][:], in0=inv[d][:], in1=gam[:, 2 * d : 2 * d + 2], op=ALU.mult)
            for n in range(2):
                nc.vector.scalar_tensor_tensor(
                    out=bb[d][:, n : n + 1], in0=mg[d][:, n : n + 1], scalar=inv[d][:, n : n + 1],
                    in1=bet_f[:, 2 * d + n : 2 * d + n + 1], op0=ALU.mult, op1=ALU.add,
                )

        def norm_v(dst, z, t):
            nc.vector.tensor_scalar(
                out=dst, in0=z, scalar1=scale_of(t), scalar2=bias_of(t), op0=ALU.mult, op1=ALU.add
            )

        def norm_s(dst, z, t):
            nc.scalar.activation(out=dst, in_=z, func=ACT.Relu, bias=bias_of(t), scale=scale_of(t))

        order = [LAST] + list(range(LAST))
        y_tiles = {}
        yg = {}
        yq = {}
        po = {}
        ot = {}
        halves = [slice(0, HALF), slice(HALF, TILE)]

        def new_y(s):
            y = work.tile([P, 4, TILE], BF16, name="y", tag="y", align_bytes=64)
            y_tiles[s] = y

        def norm(s, t, on, cols=slice(0, TILE)):
            if s < TILES:
                z = z_last[t] if s == 0 else zk[order[s]][:, t, :]
                on(y_tiles[s][:, t, cols], z[:, cols], t)

        def group_y(s, h):
            if (s, h) not in yg:
                g = work.tile([P, HALF, 4], BF16, name="yg%d" % h, tag="yg%d" % h, align_bytes=64)
                yg[s, h] = g
            return yg[s, h]

        def group_on_vector(s, lo, hi):
            src = y_tiles[s][:, :, lo:hi].rearrange("p t (c i) -> p c t i", i=4)
            dst = group_y(s, 0)[:, lo:hi, :].rearrange("p (c i) t -> p c t i", i=4)
            nc.vector.tensor_scalar(out=dst, in0=src, scalar1=0.0, scalar2=None, op0=ALU.max)

        def group_on_scalar(s, lo, hi):
            src = y_tiles[s][:, :, lo:hi].rearrange("p t (c i) -> p c t i", i=4)
            h = lo // HALF
            dst = group_y(s, h)[:, lo - h * HALF : hi - h * HALF, :].rearrange("p (c i) t -> p c t i", i=4)
            nc.scalar.copy(out=dst, in_=src)

        def quantize_y(s, h):
            yc = work.tile([P, HALF], U32, name="yc%d" % h, tag="yc%d" % h, align_bytes=64)
            ys = work.tile([P, HALF], U8, name="ys%d" % h, tag="ys%d" % h, align_bytes=64)
            quantize(yc[:], ys[:], yg[s, h][:])
            yq[s, h] = (yc, ys)

        def project(s, q):
            h, n = divmod(q, 2)
            yc, ys = yq[s, h]
            bank = psum.tile([P, C], F32, name="x%d" % q, tag="x%d" % q)
            nc.tensor.matmul_mx(
                out=bank[:],
                lhsT=yc[:, n * P : (n + 1) * P].bitcast(FP8X4),
                lhsT_scale=ys[:, n * P : (n + 1) * P],
                rhs=w2_codes[:].bitcast(FP8X4),
                rhs_scale=w2_scales[:],
                start=True,
                stop=True,
            )
            po[s, q] = bank

        def add_bias(s, q):
            h, n = divmod(q, 2)
            if n == 0:
                o = outp.tile([P, 2, C], F32, name="ot", tag="ot")
                ot[s, h] = o
            nc.vector.tensor_tensor(out=ot[s, h][:, n, :], in0=po[s, q][:], in1=b2_all[:], op=ALU.add)
            if s == TILES - 1:
                nc.sync.dma_start(out=out_v[order[s]][:, q : q + 1, :], in_=ot[s, h][:, n : n + 1, :])
            elif n == 1:
                nc.sync.dma_start(out=out_v[order[s]][:, 2 * h : 2 * h + 2, :], in_=ot[s, h][:])

        stat(0)
        stat(1)
        aggregate(0)
        aggregate(1)
        root(0)
        stat(2)
        shift(0)
        recip(0)
        stat(3)
        factors(0)
        aggregate(2)
        aggregate(3)
        root(1)
        new_y(0)
        new_y(1)
        norm(0, 0, norm_s)
        norm(0, 1, norm_s)
        norm(1, 0, norm_v, halves[0])
        shift(1)
        recip(1)
        norm(1, 1, norm_v, halves[0])
        factors(1)
        for t in (2, 3):
            norm(0, t, norm_v, halves[0])
            norm(0, t, norm_s, halves[1])

        group_on_scalar(0, HALF, TILE)
        norm(1, 2, norm_v, halves[0])
        group_on_vector(0, 0, HALF)
        norm(1, 3, norm_v, halves[0])
        for t in range(4):
            norm(1, t, norm_s, halves[1])
        quantize_y(0, 0)
        project(0, 0)
        project(0, 1)
        group_on_vector(1, 0, HALF)
        quantize_y(0, 1)
        project(0, 2)
        project(0, 3)
        add_bias(0, 0)
        add_bias(0, 1)

        for s in range(1, TILES):
            if s + 1 < TILES:
                new_y(s + 1)
            norm(s + 1, 0, norm_s)
            group_on_scalar(s, HALF, TILE)
            for t in range(1, 4):
                norm(s + 1, t, norm_s)
            if s > 1:
                group_on_vector(s, 0, HALF)
            add_bias(s - 1, 2)
            quantize_y(s, 0)
            project(s, 0)
            project(s, 1)
            add_bias(s - 1, 3)
            quantize_y(s, 1)
            project(s, 2)
            project(s, 3)
            add_bias(s, 0)
            add_bias(s, 1)
        add_bias(TILES - 1, 2)
        add_bias(TILES - 1, 3)
